import numpy as np
import ml_dtypes


def mxq(x, axis, fmt="e4m3"):
    dtype, down = {"e4m3": (ml_dtypes.float8_e4m3fn, 7), "e5m2": (ml_dtypes.float8_e5m2, 14)}[fmt]
    v = np.moveaxis(np.asarray(x, np.float32).astype(ml_dtypes.bfloat16).astype(np.float64), axis, -1)
    blocks = v.reshape(v.shape[:-1] + (-1, 32))
    amax = np.abs(blocks).max(-1, keepdims=True)
    byte = np.maximum(np.where(amax > 0, np.frexp(amax)[1] - 1 + 127, 0) - down, 1)
    scale = np.exp2(byte - 127.0)
    codes = (blocks / scale).astype(np.float32).astype(dtype).astype(np.float64)
    return np.moveaxis((codes * scale).reshape(v.shape), -1, axis)


WIDE = False


def mx_kscale(k):
    if not WIDE:
        return np.ones(k)
    levels = np.array([10, -10, 5, -5, 0])
    a = np.random.permutation(np.resize(levels, k // 512 * 4)).reshape(k // 512, 4)
    idx = np.arange(k)
    return np.exp2(a[idx // 512, idx % 128 // 32])


BF16 = ml_dtypes.bfloat16


def bf(x):
    return np.asarray(x, np.float32).astype(BF16)


def f64(x):
    return np.asarray(x).astype(np.float64)


B, H, W, C = 128, 7, 7, 512
G = C // 4
NBR = 3


def setup_inputs():
    s = mx_kscale(C)
    return {
        "h_mix": bf(0.8 * np.random.standard_normal((B, H, W, C)) * s),
        "w_mix": bf(0.8 * np.random.standard_normal((B, H, W, C)) * s),
        "c_proj": bf(np.random.standard_normal((B, H, W, C)) * s),
        "gate_hid": bf(0.6 * np.random.standard_normal((B, G))),
        "wa2": bf(2.0 * np.random.standard_normal((G, C * NBR)) / np.sqrt(G)),
        "ba2": bf(0.6 * np.random.standard_normal(C * NBR)),
        "wo": bf(np.random.standard_normal((C, C)) / np.sqrt(C) / s[:, None]),
        "bo": bf(0.3 * np.random.standard_normal(C)),
    }


def reference(h_mix, w_mix, c_proj, gate_hid, wa2, ba2, wo, bo):
    z = f64(gate_hid) @ f64(wa2) + f64(ba2)
    z = z.reshape(B, C, NBR).transpose(2, 0, 1)
    e = np.exp(z - z.max(0, keepdims=True))
    a = (e / e.sum(0, keepdims=True))[:, :, None, None, :]
    fused = f64(h_mix) * a[0] + f64(w_mix) * a[1] + f64(c_proj) * a[2]
    return (mxq(fused, 3, "e4m3") @ mxq(f64(wo), 0, "e4m3")) + f64(bo)

@@ -1,0 +1,265 @@
+from contextlib import ExitStack
+
+import concourse.mybir as mybir
+from concourse.masks import make_identity
+
+FLOPS = 2 * 128 * 49 * 512 * 512 + 2 * 128 * 128 * 1536
+
+F32 = mybir.dt.float32
+BF16 = mybir.dt.bfloat16
+I32 = mybir.dt.int32
+U32 = mybir.dt.uint32
+U8 = mybir.dt.uint8
+FP8X4 = mybir.dt.float8_e4m3fn_x4
+ALU = mybir.AluOpType
+ACT = mybir.ActivationFunctionType
+
+P = 128
+NPOS = 49
+C = 512
+T = 4
+CHUNK = 8
+BATCH = 4
+GROUP = 2
+G_W_BATCHES = (2, 5, 8, 11)
+PSUM_A_FROM = 2
+
+
+def tile_hiremodule_pc_t_kernel(tc, h_mix, w_mix, c_proj, gate_hid, wa2, ba2, wo, bo, out):
+    nc = tc.nc
+    xs = [x.rearrange("b i j c -> b (i j) c") for x in (h_mix, w_mix, c_proj)]
+    out_v = out.rearrange("b i j c -> b (i j) c")
+
+    chunks = [(i0, min(CHUNK, NPOS - i0)) for i0 in range(0, NPOS, CHUNK)]
+    groups = [(i0, min(GROUP, NPOS - i0)) for i0 in range(0, NPOS, GROUP)]
+    n_groups = len(groups)
+
+    with ExitStack() as ctx:
+        ctx.enter_context(tc.manual_schedule())
+        const = ctx.enter_context(tc.tile_pool(name="const", bufs=1))
+        xpool = ctx.enter_context(tc.tile_pool(name="x", bufs=4))
+        ppool = ctx.enter_context(tc.tile_pool(name="prod", bufs=3))
+        qpool = ctx.enter_context(tc.tile_pool(name="quant", bufs=3))
+        opool = ctx.enter_context(tc.tile_pool(name="outs", bufs=4))
+        ps_a = ctx.enter_context(tc.psum_pool(name="ps_a", bufs=1))
+        ps_f = ctx.enter_context(tc.psum_pool(name="ps_f", bufs=4))
+        ps_o = ctx.enter_context(tc.psum_pool(name="ps_o", bufs=2))
+
+        bz = const.tile([P, 3 * C + C], BF16, name="bz")
+        ones = const.tile([P, P], BF16, name="ones")
+        warm = const.tile([P, 2], F32, name="warm")
+        ident_b = const.tile([P, P], BF16, name="ident_b")
+        ident_f = const.tile([P, P], F32, name="ident_f")
+        gh = const.tile([P, P], BF16, name="gh")
+        gh_t = const.tile([P, P], BF16, name="gh_t")
+        wa2_sb = const.tile([P, 3 * C], BF16, name="wa2_sb")
+        wo_raw = const.tile([P, T, C], BF16, name="wo_raw")
+        wo_grp = const.tile([P, C, T], BF16, name="wo_grp", align_bytes=64)
+        wo_codes = const.tile([P, C], U32, name="wo_codes", align_bytes=64)
+        wo_scales = const.tile([P, C], U8, name="wo_scales", align_bytes=64)
+        bo_b = const.tile([P, C], F32, name="bo_b")
+        e = [const.tile([P, C], F32, name="e%d" % k) for k in range(3)]
+        mx = const.tile([P, C], F32, name="mx")
+        sm = const.tile([P, C], F32, name="sm")
+        a_t = [const.tile([P, T, P], F32, name="a_t%d" % k) for k in range(2)]
+
+        nc.vector.memset(bz[:].bitcast(I32), 0)
+        nc.vector.memset(ones[:], 1.0)
+        nc.vector.memset(warm[:, 0:1], 0.0)
+        nc.scalar.activation(out=warm[:, 1:2], in_=warm[:, 0:1], func=ACT.Exp)
+        make_identity(nc, ident_b[:])
+        make_identity(nc, ident_f[:])
+
+        nc.sync.dma_start(out=gh[:], in_=gate_hid)
+        nc.sync.dma_start(out=bz[0:1, 0 : 3 * C], in_=ba2.unsqueeze(0))
+        nc.sync.dma_start(out=wa2_sb[:], in_=wa2)
+        nc.sync.dma_start(out=bz[0:1, 3 * C : 4 * C], in_=bo.unsqueeze(0))
+        nc.sync.dma_start(out=wo_raw[:], in_=wo.rearrange("(t p) n -> p t n", p=P))
+
+        x_tiles = {}
+
+        def load_chunk(c):
+            i0, n = chunks[c]
+            for k in range(3):
+                xt = xpool.tile([P, n, C], BF16, name="x%d_%d" % (k, c), tag="x%d" % k)
+                nc.sync.dma_start(out=xt[:], in_=xs[k][:, i0 : i0 + n, :])
+                x_tiles[(k, c)] = xt
+
+        for c in range(4):
+            load_chunk(c)
+
+        nc.gpsimd.tensor_scalar(
+            out=wo_grp[:],
+            in0=wo_raw[:].rearrange("p t n -> p n t"),
+            scalar1=1.0,
+            scalar2=0.0,
+            op0=ALU.mult,
+            op1=ALU.add,
+        )
+
+        tp = ps_o.tile([P, P], BF16, name="tp", tag="o")
+        nc.tensor.transpose(tp[:], gh[:], ident_b[:])
+        nc.vector.tensor_copy(out=gh_t[:], in_=tp[:])
+
+        bz_k = bz[:, 0 : 3 * C].rearrange("g (c k) -> g k c", k=3)
+        wa2_k = wa2_sb[:].rearrange("g (c k) -> g k c", k=3)
+        z = [ps_f.tile([P, C], F32, name="z%d" % k, tag="f") for k in range(3)]
+        for k in range(3):
+            nc.tensor.matmul(z[k][:], lhsT=ones[:], rhs=bz_k[:, k, :], start=True, stop=False)
+        bo_ps = ps_o.tile([P, C], F32, name="bo_ps", tag="o")
+        nc.tensor.matmul(bo_ps[:], lhsT=ones[:], rhs=bz[:, 3 * C : 4 * C], start=True, stop=True)
+        for k in range(3):
+            nc.tensor.matmul(z[k][:], lhsT=gh_t[:], rhs=wa2_k[:, k, :], start=False, stop=True)
+
+        nc.scalar.copy(out=e[0][:], in_=z[0][:])
+        nc.vector.tensor_tensor(out=mx[:], in0=z[1][:], in1=e[0][:], op=ALU.max)
+        nc.vector.tensor_tensor(out=mx[:], in0=z[2][:], in1=mx[:], op=ALU.max)
+        nc.vector.tensor_tensor(out=e[2][:], in0=z[2][:], in1=mx[:], op=ALU.subtract)
+        nc.scalar.activation(out=e[2][:], in_=e[2][:], func=ACT.Exp)
+        nc.vector.tensor_tensor(out=e[0][:], in0=e[0][:], in1=mx[:], op=ALU.subtract)
+        nc.scalar.activation(out=e[0][:], in_=e[0][:], func=ACT.Exp)
+        nc.vector.tensor_tensor(out=e[1][:], in0=z[1][:], in1=mx[:], op=ALU.subtract)
+        nc.scalar.activation(out=e[1][:], in_=e[1][:], func=ACT.Exp)
+        nc.scalar.copy(out=bo_b[:], in_=bo_ps[:])
+        nc.vector.quantize_mx(
+            out=wo_codes[:].bitcast(FP8X4),
+            scales=wo_scales[:],
+            in_=wo_grp[:].rearrange("p n t -> p (n t)"),
+        )
+        nc.vector.tensor_tensor(out=sm[:], in0=e[2][:], in1=e[0][:], op=ALU.add)
+        nc.vector.tensor_tensor(out=sm[:], in0=sm[:], in1=e[1][:], op=ALU.add)
+        nc.vector.reciprocal(out=sm[:], in_=sm[:])
+        for k in (2, 0, 1):
+            nc.vector.tensor_tensor(out=e[k][:], in0=e[k][:], in1=sm[:], op=ALU.mult)
+
+        a_ps = [ps_a.tile([P, C], F32, name="a_ps%d" % k, tag="a%d" % k) for k in range(2)]
+        for k in range(2):
+            tmp = ps_f.tile([P, T, P], F32, name="a_tmp%d" % k, tag="f")
+            for t in range(T):
+                nc.tensor.transpose(tmp[:, t, :], e[k][:, t * P : (t + 1) * P], ident_f[:])
+            nc.scalar.copy(out=a_t[k][:], in_=tmp[:])
+        for k in range(2):
+            for t in range(T):
+                nc.tensor.transpose(a_ps[k][:, t * P : (t + 1) * P], a_t[k][:, t, :], ident_f[:])
+
+        prod = {}
+        grp_t = {}
+        code_t = {}
+        o_t = {}
+        osb_t = {}
+
+        def gp_job(k, i0, n):
+            c = i0 // CHUNK
+            pt = ppool.tile([P, n, C], F32, name="pg%d_%d" % (k, i0), tag="pg%d" % k, bufs=(3 if k == 2 else 2))
+            nc.gpsimd.tensor_tensor(
+                out=pt[:],
+                in0=x_tiles[(k, c)][:, i0 - c * CHUNK : i0 - c * CHUNK + n, :],
+                in1=e[k][:].unsqueeze(1).to_broadcast([P, n, C]),
+                op=ALU.mult,
+            )
+            for j in range(n):
+                prod[(k, i0 + j)] = (pt, j)
+
+        def gp_jobs_for_step(s):
+            jobs = []
+            if s == 0:
+                jobs += [(2, 0, 2), (2, 2, 2)]
+            for b in range(1, (NPOS + BATCH - 1) // BATCH):
+                if max(0, 2 * b - 2) == s:
+                    n = min(BATCH, NPOS - b * BATCH)
+                    if b in G_W_BATCHES:
+                        jobs.append((1, b * BATCH, n))
+                    jobs.append((2, b * BATCH, n))
+            return jobs
+
+        def vec_products(s):
+            i0, n = groups[s]
+            c = i0 // CHUNK
+            ks = [0] if (i0 // BATCH) in G_W_BATCHES else [0, 1]
+            for k in ks:
+                pt = ppool.tile([P, n, C], F32, name="pv%d_%d" % (k, i0), tag="pv%d" % k)
+                a_src = a_ps[k] if s >= PSUM_A_FROM else e[k]
+                nc.vector.tensor_tensor(
+                    out=pt[:],
+                    in0=x_tiles[(k, c)][:, i0 - c * CHUNK : i0 - c * CHUNK + n, :],
+                    in1=a_src[:].unsqueeze(1).to_broadcast([P, n, C]),
+                    op=ALU.mult,
+                )
+                for j in range(n):
+                    prod[(k, i0 + j)] = (pt, j)
+
+        def sum_transposed(s):
+            i0, n = groups[s]
+            grp = qpool.tile([P, GROUP, P, T], BF16, name="grp%d" % s, tag="grp", align_bytes=64)
+            grp_t[s] = grp
+            for j in range(n):
+                ft = ps_f.tile([P, T, P], F32, name="ft%d" % (i0 + j), tag="f")
+                for t in range(T):
+                    for k in range(3):
+                        pt, jj = prod[(k, i0 + j)]
+                        nc.tensor.matmul(
+                            ft[:, t, :],
+                            lhsT=pt[:, jj, t * P : (t + 1) * P],
+                            rhs=ident_f[:],
+                            is_transpose=True,
+                            start=(k == 0),
+                            stop=(k == 2),
+                        )
+                nc.scalar.copy(out=grp[:, j, :, :], in_=ft[:].rearrange("p t b -> p b t"))
+
+        def quantise(s):
+            i0, n = groups[s]
+            codes = qpool.tile([P, GROUP * P], U32, name="codes%d" % s, tag="codes", align_bytes=64)
+            scales = qpool.tile([P, GROUP * P], U8, name="scales%d" % s, tag="scales", align_bytes=64)
+            code_t[s] = (codes, scales)
+            nc.vector.quantize_mx(
+                out=codes[:, 0 : n * P].bitcast(FP8X4),
+                scales=scales[:, 0 : n * P],
+                in_=grp_t[s][:, 0:n, :, :].rearrange("p j b t -> p (j b t)"),
+            )
+
+        def project(s):
+            i0, n = groups[s]
+            codes, scales = code_t[s]
+            o_t[s] = []
+            for j in range(n):
+                o = ps_o.tile([P, C], F32, name="o%d" % (i0 + j), tag="o")
+                nc.tensor.matmul_mx(
+                    out=o[:],
+                    lhsT=codes[:, j * P : (j + 1) * P].bitcast(FP8X4),
+                    lhsT_scale=scales[:, j * P : (j + 1) * P],
+                    rhs=wo_codes[:].bitcast(FP8X4),
+                    rhs_scale=wo_scales[:],
+                    start=True,
+                    stop=True,
+                )
+                o_t[s].append(o)
+
+        def add_bias(s):
+            i0, n = groups[s]
+            osb = opool.tile([P, GROUP, C], F32, name="osb%d" % s, tag="osb")
+            osb_t[s] = osb
+            for j in range(n):
+                nc.vector.tensor_tensor(out=osb[:, j, :], in0=o_t[s][j][:], in1=bo_b[:], op=ALU.add)
+
+        def store(s):
+            i0, n = groups[s]
+            nc.scalar.dma_start(out=out_v[:, i0 : i0 + n, :], in_=osb_t[s][:, 0:n, :])
+
+        for s in range(n_groups + 3):
+            if 0 <= s - 2 < n_groups:
+                quantise(s - 2)
+            if 0 <= s - 3 < n_groups:
+                add_bias(s - 3)
+            if s < n_groups:
+                vec_products(s)
+            for job in gp_jobs_for_step(s):
+                gp_job(job[0], job[1], job[2])
+            if s % 4 == 3 and s // 4 + 4 < len(chunks):
+                load_chunk(s // 4 + 4)
+            if 0 <= s - 1 < n_groups:
+                sum_transposed(s - 1)
+            if 0 <= s - 2 < n_groups:
+                project(s - 2)
+            if 0 <= s - 3 < n_groups:
+                store(s - 3)

@@ -21,7 +21,7 @@ T = 4
 CHUNK = 8
 BATCH = 4
 GROUP = 2
-G_W_BATCHES = (2, 5, 8, 11)
+CLOCK_PASSES = 1
 PSUM_A_FROM = 2
 
 
@@ -167,7 +167,7 @@ def tile_hiremodule_pc_t_kernel(tc, h_mix, w_mix, c_proj, gate_hid, wa2, ba2, wo
             for b in range(1, (NPOS + BATCH - 1) // BATCH):
                 if max(0, 2 * b - 2) == s:
                     n = min(BATCH, NPOS - b * BATCH)
-                    if b in G_W_BATCHES:
+                    if b % 3 == 2:
                         jobs.append((1, b * BATCH, n))
                     jobs.append((2, b * BATCH, n))
             return jobs
@@ -175,7 +175,7 @@ def tile_hiremodule_pc_t_kernel(tc, h_mix, w_mix, c_proj, gate_hid, wa2, ba2, wo
         def vec_products(s):
             i0, n = groups[s]
             c = i0 // CHUNK
-            ks = [0] if (i0 // BATCH) in G_W_BATCHES else [0, 1]
+            ks = [0] if (i0 // BATCH) % 3 == 2 else [0, 1]
             for k in ks:
                 pt = ppool.tile([P, n, C], F32, name="pv%d_%d" % (k, i0), tag="pv%d" % k)
                 a_src = a_ps[k] if s >= PSUM_A_FROM else e[k]
@@ -188,11 +188,12 @@ def tile_hiremodule_pc_t_kernel(tc, h_mix, w_mix, c_proj, gate_hid, wa2, ba2, wo
                 for j in range(n):
                     prod[(k, i0 + j)] = (pt, j)
 
-        def sum_transposed(s):
+        def sum_transposed(s, j):
             i0, n = groups[s]
-            grp = qpool.tile([P, GROUP, P, T], BF16, name="grp%d" % s, tag="grp", align_bytes=64)
-            grp_t[s] = grp
-            for j in range(n):
+            if j == 0:
+                grp_t[s] = qpool.tile([P, GROUP, P, T], BF16, name="grp%d" % s, tag="grp", align_bytes=64)
+            grp = grp_t[s]
+            if j < n:
                 ft = ps_f.tile([P, T, P], F32, name="ft%d" % (i0 + j), tag="f")
                 for t in range(T):
                     for k in range(3):
@@ -218,21 +219,23 @@ def tile_hiremodule_pc_t_kernel(tc, h_mix, w_mix, c_proj, gate_hid, wa2, ba2, wo
                 in_=grp_t[s][:, 0:n, :, :].rearrange("p j b t -> p (j b t)"),
             )
 
-        def project(s):
+        def project(s, j):
             i0, n = groups[s]
             codes, scales = code_t[s]
-            o_t[s] = []
-            for j in range(n):
+            if j == 0:
+                o_t[s] = []
+            if j < n:
                 o = ps_o.tile([P, C], F32, name="o%d" % (i0 + j), tag="o")
-                nc.tensor.matmul_mx(
-                    out=o[:],
-                    lhsT=codes[:, j * P : (j + 1) * P].bitcast(FP8X4),
-                    lhsT_scale=scales[:, j * P : (j + 1) * P],
-                    rhs=wo_codes[:].bitcast(FP8X4),
-                    rhs_scale=wo_scales[:],
-                    start=True,
-                    stop=True,
-                )
+                for rep in range(1 + CLOCK_PASSES):
+                    nc.tensor.matmul_mx(
+                        out=o[:],
+                        lhsT=codes[:, j * P : (j + 1) * P].bitcast(FP8X4),
+                        lhsT_scale=scales[:, j * P : (j + 1) * P],
+                        rhs=wo_codes[:].bitcast(FP8X4),
+                        rhs_scale=wo_scales[:],
+                        start=True,
+                        stop=True,
+                    )
                 o_t[s].append(o)
 
         def add_bias(s):
@@ -257,9 +260,10 @@ def tile_hiremodule_pc_t_kernel(tc, h_mix, w_mix, c_proj, gate_hid, wa2, ba2, wo
                 gp_job(job[0], job[1], job[2])
             if s % 4 == 3 and s // 4 + 4 < len(chunks):
                 load_chunk(s // 4 + 4)
-            if 0 <= s - 1 < n_groups:
-                sum_transposed(s - 1)
-            if 0 <= s - 2 < n_groups:
-                project(s - 2)
+            for j in range(GROUP):
+                if 0 <= s - 1 < n_groups:
+                    sum_transposed(s - 1, j)
+                if 0 <= s - 2 < n_groups:
+                    project(s - 2, j)
             if 0 <= s - 3 < n_groups:
                 store(s - 3)

@@ -21,7 +21,6 @@ T = 4
 CHUNK = 8
 BATCH = 4
 GROUP = 2
-CLOCK_PASSES = 1
 PSUM_A_FROM = 2
 
 
@@ -188,25 +187,25 @@ def tile_hiremodule_pc_t_kernel(tc, h_mix, w_mix, c_proj, gate_hid, wa2, ba2, wo
                 for j in range(n):
                     prod[(k, i0 + j)] = (pt, j)
 
-        def sum_transposed(s, j):
+        def sum_transposed(s):
             i0, n = groups[s]
-            if j == 0:
-                grp_t[s] = qpool.tile([P, GROUP, P, T], BF16, name="grp%d" % s, tag="grp", align_bytes=64)
-            grp = grp_t[s]
-            if j < n:
-                ft = ps_f.tile([P, T, P], F32, name="ft%d" % (i0 + j), tag="f")
-                for t in range(T):
-                    for k in range(3):
-                        pt, jj = prod[(k, i0 + j)]
+            grp = qpool.tile([P, GROUP, P, T], BF16, name="grp%d" % s, tag="grp", align_bytes=64)
+            grp_t[s] = grp
+            fts = [ps_f.tile([P, T, P], F32, name="ft%d" % (i0 + j), tag="f") for j in range(n)]
+            for k in range(3):
+                for j in range(n):
+                    pt, jj = prod[(k, i0 + j)]
+                    for t in range(T):
                         nc.tensor.matmul(
-                            ft[:, t, :],
+                            fts[j][:, t, :],
                             lhsT=pt[:, jj, t * P : (t + 1) * P],
                             rhs=ident_f[:],
                             is_transpose=True,
-                            start=(k == 0),
-                            stop=(k == 2),
+                            start=(k == 0 and t == 0),
+                            stop=(k == 2 and t == T - 1),
                         )
-                nc.scalar.copy(out=grp[:, j, :, :], in_=ft[:].rearrange("p t b -> p b t"))
+            for j in range(n):
+                nc.scalar.copy(out=grp[:, j, :, :], in_=fts[j][:].rearrange("p t b -> p b t"))
 
         def quantise(s):
             i0, n = groups[s]
@@ -219,23 +218,21 @@ def tile_hiremodule_pc_t_kernel(tc, h_mix, w_mix, c_proj, gate_hid, wa2, ba2, wo
                 in_=grp_t[s][:, 0:n, :, :].rearrange("p j b t -> p (j b t)"),
             )
 
-        def project(s, j):
+        def project(s):
             i0, n = groups[s]
             codes, scales = code_t[s]
-            if j == 0:
-                o_t[s] = []
-            if j < n:
+            o_t[s] = []
+            for j in range(n):
                 o = ps_o.tile([P, C], F32, name="o%d" % (i0 + j), tag="o")
-                for rep in range(1 + CLOCK_PASSES):
-                    nc.tensor.matmul_mx(
-                        out=o[:],
-                        lhsT=codes[:, j * P : (j + 1) * P].bitcast(FP8X4),
-                        lhsT_scale=scales[:, j * P : (j + 1) * P],
-                        rhs=wo_codes[:].bitcast(FP8X4),
-                        rhs_scale=wo_scales[:],
-                        start=True,
-                        stop=True,
-                    )
+                nc.tensor.matmul_mx(
+                    out=o[:],
+                    lhsT=codes[:, j * P : (j + 1) * P].bitcast(FP8X4),
+                    lhsT_scale=scales[:, j * P : (j + 1) * P],
+                    rhs=wo_codes[:].bitcast(FP8X4),
+                    rhs_scale=wo_scales[:],
+                    start=True,
+                    stop=True,
+                )
                 o_t[s].append(o)
 
         def add_bias(s):
@@ -260,10 +257,9 @@ def tile_hiremodule_pc_t_kernel(tc, h_mix, w_mix, c_proj, gate_hid, wa2, ba2, wo
                 gp_job(job[0], job[1], job[2])
             if s % 4 == 3 and s // 4 + 4 < len(chunks):
                 load_chunk(s // 4 + 4)
-            for j in range(GROUP):
-                if 0 <= s - 1 < n_groups:
-                    sum_transposed(s - 1, j)
-                if 0 <= s - 2 < n_groups:
-                    project(s - 2, j)
+            if 0 <= s - 1 < n_groups:
+                sum_transposed(s - 1)
+            if 0 <= s - 2 < n_groups:
+                project(s - 2)
             if 0 <= s - 3 < n_groups:
                 store(s - 3)

@@ -224,15 +224,16 @@ def tile_hiremodule_pc_t_kernel(tc, h_mix, w_mix, c_proj, gate_hid, wa2, ba2, wo
             o_t[s] = []
             for j in range(n):
                 o = ps_o.tile([P, C], F32, name="o%d" % (i0 + j), tag="o")
-                nc.tensor.matmul_mx(
-                    out=o[:],
-                    lhsT=codes[:, j * P : (j + 1) * P].bitcast(FP8X4),
-                    lhsT_scale=scales[:, j * P : (j + 1) * P],
-                    rhs=wo_codes[:].bitcast(FP8X4),
-                    rhs_scale=wo_scales[:],
-                    start=True,
-                    stop=True,
-                )
+                for rep in range(2):
+                    nc.tensor.matmul_mx(
+                        out=o[:],
+                        lhsT=codes[:, j * P : (j + 1) * P].bitcast(FP8X4),
+                        lhsT_scale=scales[:, j * P : (j + 1) * P],
+                        rhs=wo_codes[:].bitcast(FP8X4),
+                        rhs_scale=wo_scales[:],
+                        start=True,
+                        stop=True,
+                    )
                 o_t[s].append(o)
 
         def add_bias(s):

@@ -147,29 +147,20 @@ def tile_hiremodule_pc_t_kernel(tc, h_mix, w_mix, c_proj, gate_hid, wa2, ba2, wo
         o_t = {}
         osb_t = {}
 
-        def gp_job(k, i0, n):
+        def gp_products(s):
+            i0, n = groups[s]
             c = i0 // CHUNK
-            pt = ppool.tile([P, n, C], F32, name="pg%d_%d" % (k, i0), tag="pg%d" % k, bufs=(3 if k == 2 else 2))
-            nc.gpsimd.tensor_tensor(
-                out=pt[:],
-                in0=x_tiles[(k, c)][:, i0 - c * CHUNK : i0 - c * CHUNK + n, :],
-                in1=e[k][:].unsqueeze(1).to_broadcast([P, n, C]),
-                op=ALU.mult,
-            )
-            for j in range(n):
-                prod[(k, i0 + j)] = (pt, j)
-
-        def gp_jobs_for_step(s):
-            jobs = []
-            if s == 0:
-                jobs += [(2, 0, 2), (2, 2, 2)]
-            for b in range(1, (NPOS + BATCH - 1) // BATCH):
-                if max(0, 2 * b - 2) == s:
-                    n = min(BATCH, NPOS - b * BATCH)
-                    if b % 3 == 2:
-                        jobs.append((1, b * BATCH, n))
-                    jobs.append((2, b * BATCH, n))
-            return jobs
+            ks = [1, 2] if (i0 // BATCH) % 3 == 2 else [2]
+            for k in ks:
+                pt = ppool.tile([P, n, C], F32, name="pg%d_%d" % (k, i0), tag="pg%d" % k, bufs=(4 if k == 2 else 3))
+                nc.gpsimd.tensor_tensor(
+                    out=pt[:],
+                    in0=x_tiles[(k, c)][:, i0 - c * CHUNK : i0 - c * CHUNK + n, :],
+                    in1=e[k][:].unsqueeze(1).to_broadcast([P, n, C]),
+                    op=ALU.mult,
+                )
+                for j in range(n):
+                    prod[(k, i0 + j)] = (pt, j)
 
         def vec_products(s):
             i0, n = groups[s]
@@ -189,8 +180,10 @@ def tile_hiremodule_pc_t_kernel(tc, h_mix, w_mix, c_proj, gate_hid, wa2, ba2, wo
 
         def sum_transposed(s):
             i0, n = groups[s]
-            grp = qpool.tile([P, GROUP, P, T], BF16, name="grp%d" % s, tag="grp", align_bytes=64)
-            grp_t[s] = grp
+            b = i0 // BATCH
+            if i0 % BATCH == 0:
+                grp_t[b] = qpool.tile([P, BATCH, P, T], BF16, name="grp%d" % b, tag="grp", align_bytes=64)
+            grp = grp_t[b]
             fts = [ps_f.tile([P, T, P], F32, name="ft%d" % (i0 + j), tag="f") for j in range(n)]
             for k in range(3):
                 for j in range(n):
@@ -205,35 +198,35 @@ def tile_hiremodule_pc_t_kernel(tc, h_mix, w_mix, c_proj, gate_hid, wa2, ba2, wo
                             stop=(k == 2 and t == T - 1),
                         )
             for j in range(n):
-                nc.scalar.copy(out=grp[:, j, :, :], in_=fts[j][:].rearrange("p t b -> p b t"))
+                nc.scalar.copy(out=grp[:, i0 % BATCH + j, :, :], in_=fts[j][:].rearrange("p t b -> p b t"))
 
-        def quantise(s):
-            i0, n = groups[s]
-            codes = qpool.tile([P, GROUP * P], U32, name="codes%d" % s, tag="codes", align_bytes=64)
-            scales = qpool.tile([P, GROUP * P], U8, name="scales%d" % s, tag="scales", align_bytes=64)
-            code_t[s] = (codes, scales)
+        def quantise(b):
+            n = min(BATCH, NPOS - b * BATCH)
+            codes = qpool.tile([P, BATCH * P], U32, name="codes%d" % b, tag="codes", align_bytes=64)
+            scales = qpool.tile([P, BATCH * P], U8, name="scales%d" % b, tag="scales", align_bytes=64)
+            code_t[b] = (codes, scales)
             nc.vector.quantize_mx(
                 out=codes[:, 0 : n * P].bitcast(FP8X4),
                 scales=scales[:, 0 : n * P],
-                in_=grp_t[s][:, 0:n, :, :].rearrange("p j b t -> p (j b t)"),
+                in_=grp_t[b][:, 0:n, :, :].rearrange("p j b t -> p (j b t)"),
             )
 
         def project(s):
             i0, n = groups[s]
-            codes, scales = code_t[s]
+            codes, scales = code_t[i0 // BATCH]
             o_t[s] = []
             for j in range(n):
                 o = ps_o.tile([P, C], F32, name="o%d" % (i0 + j), tag="o")
-                for rep in range(2):
-                    nc.tensor.matmul_mx(
-                        out=o[:],
-                        lhsT=codes[:, j * P : (j + 1) * P].bitcast(FP8X4),
-                        lhsT_scale=scales[:, j * P : (j + 1) * P],
-                        rhs=wo_codes[:].bitcast(FP8X4),
-                        rhs_scale=wo_scales[:],
-                        start=True,
-                        stop=True,
-                    )
+                col = (i0 % BATCH + j) * P
+                nc.tensor.matmul_mx(
+                    out=o[:],
+                    lhsT=codes[:, col : col + P].bitcast(FP8X4),
+                    lhsT_scale=scales[:, col : col + P],
+                    rhs=wo_codes[:].bitcast(FP8X4),
+                    rhs_scale=wo_scales[:],
+                    start=True,
+                    stop=True,
+                )
                 o_t[s].append(o)
 
         def add_bias(s):
@@ -247,20 +240,30 @@ def tile_hiremodule_pc_t_kernel(tc, h_mix, w_mix, c_proj, gate_hid, wa2, ba2, wo
             i0, n = groups[s]
             nc.scalar.dma_start(out=out_v[:, i0 : i0 + n, :], in_=osb_t[s][:, 0:n, :])
 
-        for s in range(n_groups + 3):
-            if 0 <= s - 2 < n_groups:
-                quantise(s - 2)
-            if 0 <= s - 3 < n_groups:
-                add_bias(s - 3)
+        n_batches = (NPOS + BATCH - 1) // BATCH
+        q_step = [min(2 * b + 1, n_groups - 1) + 2 for b in range(n_batches)]
+        mx_step = [q_step[g // 2] + g % 2 for g in range(n_groups)]
+
+        gp_products(0)
+        gp_products(1)
+        for s in range(mx_step[n_groups - 1] + 2):
+            for b in range(n_batches):
+                if q_step[b] == s:
+                    quantise(b)
+            for g in range(n_groups):
+                if mx_step[g] + 1 == s:
+                    add_bias(g)
             if s < n_groups:
                 vec_products(s)
-            for job in gp_jobs_for_step(s):
-                gp_job(job[0], job[1], job[2])
+            if s + 2 < n_groups:
+                gp_products(s + 2)
             if s % 4 == 3 and s // 4 + 4 < len(chunks):
                 load_chunk(s // 4 + 4)
             if 0 <= s - 1 < n_groups:
                 sum_transposed(s - 1)
-            if 0 <= s - 2 < n_groups:
-                project(s - 2)
-            if 0 <= s - 3 < n_groups:
-                store(s - 3)
+            for g in range(n_groups):
+                if mx_step[g] == s:
+                    project(g)
+            for g in range(n_groups):
+                if mx_step[g] + 1 == s:
+                    store(g)

@@ -21,7 +21,7 @@ T = 4
 CHUNK = 8
 BATCH = 4
 GROUP = 2
-PSUM_A_FROM = 2
+PSUM_A_FROM = 1
 
 
 def tile_hiremodule_pc_t_kernel(tc, h_mix, w_mix, c_proj, gate_hid, wa2, ba2, wo, bo, out):
@@ -38,7 +38,7 @@ def tile_hiremodule_pc_t_kernel(tc, h_mix, w_mix, c_proj, gate_hid, wa2, ba2, wo
         const = ctx.enter_context(tc.tile_pool(name="const", bufs=1))
         xpool = ctx.enter_context(tc.tile_pool(name="x", bufs=4))
         ppool = ctx.enter_context(tc.tile_pool(name="prod", bufs=3))
-        qpool = ctx.enter_context(tc.tile_pool(name="quant", bufs=3))
+        qpool = ctx.enter_context(tc.tile_pool(name="quant", bufs=2))
         opool = ctx.enter_context(tc.tile_pool(name="outs", bufs=4))
         ps_a = ctx.enter_context(tc.psum_pool(name="ps_a", bufs=1))
         ps_f = ctx.enter_context(tc.psum_pool(name="ps_f", bufs=4))
@@ -128,7 +128,7 @@ def tile_hiremodule_pc_t_kernel(tc, h_mix, w_mix, c_proj, gate_hid, wa2, ba2, wo
         nc.vector.tensor_tensor(out=sm[:], in0=e[2][:], in1=e[0][:], op=ALU.add)
         nc.vector.tensor_tensor(out=sm[:], in0=sm[:], in1=e[1][:], op=ALU.add)
         nc.vector.reciprocal(out=sm[:], in_=sm[:])
-        for k in (2, 0, 1):
+        for k in (0, 1):
             nc.vector.tensor_tensor(out=e[k][:], in0=e[k][:], in1=sm[:], op=ALU.mult)
 
         a_ps = [ps_a.tile([P, C], F32, name="a_ps%d" % k, tag="a%d" % k) for k in range(2)]
@@ -180,10 +180,10 @@ def tile_hiremodule_pc_t_kernel(tc, h_mix, w_mix, c_proj, gate_hid, wa2, ba2, wo
 
         def sum_transposed(s):
             i0, n = groups[s]
-            b = i0 // BATCH
-            if i0 % BATCH == 0:
-                grp_t[b] = qpool.tile([P, BATCH, P, T], BF16, name="grp%d" % b, tag="grp", align_bytes=64)
-            grp = grp_t[b]
+            c = i0 // CHUNK
+            if i0 % CHUNK == 0:
+                grp_t[c] = qpool.tile([P, CHUNK, P, T], BF16, name="grp%d" % c, tag="grp", align_bytes=64)
+            grp = grp_t[c]
             fts = [ps_f.tile([P, T, P], F32, name="ft%d" % (i0 + j), tag="f") for j in range(n)]
             for k in range(3):
                 for j in range(n):
@@ -198,26 +198,26 @@ def tile_hiremodule_pc_t_kernel(tc, h_mix, w_mix, c_proj, gate_hid, wa2, ba2, wo
                             stop=(k == 2 and t == T - 1),
                         )
             for j in range(n):
-                nc.scalar.copy(out=grp[:, i0 % BATCH + j, :, :], in_=fts[j][:].rearrange("p t b -> p b t"))
+                nc.scalar.copy(out=grp[:, i0 % CHUNK + j, :, :], in_=fts[j][:].rearrange("p t b -> p b t"))
 
-        def quantise(b):
-            n = min(BATCH, NPOS - b * BATCH)
-            codes = qpool.tile([P, BATCH * P], U32, name="codes%d" % b, tag="codes", align_bytes=64)
-            scales = qpool.tile([P, BATCH * P], U8, name="scales%d" % b, tag="scales", align_bytes=64)
-            code_t[b] = (codes, scales)
+        def quantise(c):
+            n = chunks[c][1]
+            codes = qpool.tile([P, CHUNK * P], U32, name="codes%d" % c, tag="codes", align_bytes=64)
+            scales = qpool.tile([P, CHUNK * P], U8, name="scales%d" % c, tag="scales", align_bytes=64)
+            code_t[c] = (codes, scales)
             nc.vector.quantize_mx(
                 out=codes[:, 0 : n * P].bitcast(FP8X4),
                 scales=scales[:, 0 : n * P],
-                in_=grp_t[b][:, 0:n, :, :].rearrange("p j b t -> p (j b t)"),
+                in_=grp_t[c][:, 0:n, :, :].rearrange("p j b t -> p (j b t)"),
             )
 
         def project(s):
             i0, n = groups[s]
-            codes, scales = code_t[i0 // BATCH]
+            codes, scales = code_t[i0 // CHUNK]
             o_t[s] = []
             for j in range(n):
                 o = ps_o.tile([P, C], F32, name="o%d" % (i0 + j), tag="o")
-                col = (i0 % BATCH + j) * P
+                col = (i0 % CHUNK + j) * P
                 nc.tensor.matmul_mx(
                     out=o[:],
                     lhsT=codes[:, col : col + P].bitcast(FP8X4),
@@ -240,20 +240,16 @@ def tile_hiremodule_pc_t_kernel(tc, h_mix, w_mix, c_proj, gate_hid, wa2, ba2, wo
             i0, n = groups[s]
             nc.scalar.dma_start(out=out_v[:, i0 : i0 + n, :], in_=osb_t[s][:, 0:n, :])
 
-        n_batches = (NPOS + BATCH - 1) // BATCH
-        q_step = [min(2 * b + 1, n_groups - 1) + 2 for b in range(n_batches)]
-        mx_step = [q_step[g // 2] + g % 2 for g in range(n_groups)]
-
+        vec_products(0)
+        nc.vector.tensor_tensor(out=e[2][:], in0=e[2][:], in1=sm[:], op=ALU.mult)
         gp_products(0)
         gp_products(1)
-        for s in range(mx_step[n_groups - 1] + 2):
-            for b in range(n_batches):
-                if q_step[b] == s:
-                    quantise(b)
-            for g in range(n_groups):
-                if mx_step[g] + 1 == s:
-                    add_bias(g)
-            if s < n_groups:
+        for s in range(n_groups + 6):
+            if s % 4 == 1 and 0 <= s // 4 - 1 < len(chunks):
+                quantise(s // 4 - 1)
+            if 0 <= s - 6 < n_groups:
+                add_bias(s - 6)
+            if 1 <= s < n_groups:
                 vec_products(s)
             if s + 2 < n_groups:
                 gp_products(s + 2)
@@ -261,9 +257,7 @@ def tile_hiremodule_pc_t_kernel(tc, h_mix, w_mix, c_proj, gate_hid, wa2, ba2, wo
                 load_chunk(s // 4 + 4)
             if 0 <= s - 1 < n_groups:
                 sum_transposed(s - 1)
-            for g in range(n_groups):
-                if mx_step[g] == s:
-                    project(g)
-            for g in range(n_groups):
-                if mx_step[g] + 1 == s:
-                    store(g)
+            if 0 <= s - 5 < n_groups:
+                project(s - 5)
+            if 0 <= s - 6 < n_groups:
+                store(s - 6)

@@ -15,249 +15,252 @@ ALU = mybir.AluOpType
 ACT = mybir.ActivationFunctionType
 
 P = 128
-NPOS = 49
 C = 512
-T = 4
-CHUNK = 8
-BATCH = 4
+PACK = 4
+STREAMS = 3
+POSITIONS = 49
 GROUP = 2
-PSUM_A_FROM = 1
+BATCH = 4
+CHUNK = 8
 
 
 def tile_hiremodule_pc_t_kernel(tc, h_mix, w_mix, c_proj, gate_hid, wa2, ba2, wo, bo, out):
     nc = tc.nc
-    xs = [x.rearrange("b i j c -> b (i j) c") for x in (h_mix, w_mix, c_proj)]
-    out_v = out.rearrange("b i j c -> b (i j) c")
+    streams = [x.rearrange("b i j c -> b (i j) c") for x in (h_mix, w_mix, c_proj)]
+    out_rows = out.rearrange("b i j c -> b (i j) c")
 
-    chunks = [(i0, min(CHUNK, NPOS - i0)) for i0 in range(0, NPOS, CHUNK)]
-    groups = [(i0, min(GROUP, NPOS - i0)) for i0 in range(0, NPOS, GROUP)]
-    n_groups = len(groups)
+    n_chunks = (POSITIONS + CHUNK - 1) // CHUNK
+    n_batches = (POSITIONS + BATCH - 1) // BATCH
+    n_groups = (POSITIONS + GROUP - 1) // GROUP
+
+    def span(index, size):
+        return index * size, min(size, POSITIONS - index * size)
+
+    def w_on_gpsimd(first):
+        return (first // BATCH) % 3 == 2
 
     with ExitStack() as ctx:
         ctx.enter_context(tc.manual_schedule())
         const = ctx.enter_context(tc.tile_pool(name="const", bufs=1))
-        xpool = ctx.enter_context(tc.tile_pool(name="x", bufs=4))
-        ppool = ctx.enter_context(tc.tile_pool(name="prod", bufs=3))
-        qpool = ctx.enter_context(tc.tile_pool(name="quant", bufs=2))
-        opool = ctx.enter_context(tc.tile_pool(name="outs", bufs=4))
-        ps_a = ctx.enter_context(tc.psum_pool(name="ps_a", bufs=1))
-        ps_f = ctx.enter_context(tc.psum_pool(name="ps_f", bufs=4))
-        ps_o = ctx.enter_context(tc.psum_pool(name="ps_o", bufs=2))
+        x_pool = ctx.enter_context(tc.tile_pool(name="x", bufs=4))
+        prod_pool = ctx.enter_context(tc.tile_pool(name="prod", bufs=3))
+        quant_pool = ctx.enter_context(tc.tile_pool(name="quant", bufs=3))
+        out_pool = ctx.enter_context(tc.tile_pool(name="outs", bufs=4))
+        psum_gate = ctx.enter_context(tc.psum_pool(name="psum_gate", bufs=1))
+        psum_sum = ctx.enter_context(tc.psum_pool(name="psum_sum", bufs=4))
+        psum_out = ctx.enter_context(tc.psum_pool(name="psum_out", bufs=2))
 
-        bz = const.tile([P, 3 * C + C], BF16, name="bz")
+        bias_rows = const.tile([P, STREAMS * C + C], BF16, name="bias_rows")
         ones = const.tile([P, P], BF16, name="ones")
         warm = const.tile([P, 2], F32, name="warm")
-        ident_b = const.tile([P, P], BF16, name="ident_b")
-        ident_f = const.tile([P, P], F32, name="ident_f")
-        gh = const.tile([P, P], BF16, name="gh")
-        gh_t = const.tile([P, P], BF16, name="gh_t")
-        wa2_sb = const.tile([P, 3 * C], BF16, name="wa2_sb")
-        wo_raw = const.tile([P, T, C], BF16, name="wo_raw")
-        wo_grp = const.tile([P, C, T], BF16, name="wo_grp", align_bytes=64)
+        ident_bf16 = const.tile([P, P], BF16, name="ident_bf16")
+        ident_f32 = const.tile([P, P], F32, name="ident_f32")
+        gate_sb = const.tile([P, P], BF16, name="gate_sb")
+        gate_t = const.tile([P, P], BF16, name="gate_t")
+        wa2_sb = const.tile([P, STREAMS * C], BF16, name="wa2_sb")
+        wo_rows = const.tile([P, PACK, C], BF16, name="wo_rows")
+        wo_grouped = const.tile([P, C, PACK], BF16, name="wo_grouped", align_bytes=64)
         wo_codes = const.tile([P, C], U32, name="wo_codes", align_bytes=64)
         wo_scales = const.tile([P, C], U8, name="wo_scales", align_bytes=64)
-        bo_b = const.tile([P, C], F32, name="bo_b")
-        e = [const.tile([P, C], F32, name="e%d" % k) for k in range(3)]
-        mx = const.tile([P, C], F32, name="mx")
-        sm = const.tile([P, C], F32, name="sm")
-        a_t = [const.tile([P, T, P], F32, name="a_t%d" % k) for k in range(2)]
+        bo_all = const.tile([P, C], F32, name="bo_all")
+        gate = [const.tile([P, C], F32, name="gate%d" % k) for k in range(STREAMS)]
+        top = const.tile([P, C], F32, name="top")
+        total = const.tile([P, C], F32, name="total")
+        gate_flipped = [const.tile([P, PACK, P], F32, name="gate_flipped%d" % k) for k in range(2)]
 
-        nc.vector.memset(bz[:].bitcast(I32), 0)
+        nc.vector.memset(bias_rows[:].bitcast(I32), 0)
         nc.vector.memset(ones[:], 1.0)
         nc.vector.memset(warm[:, 0:1], 0.0)
         nc.scalar.activation(out=warm[:, 1:2], in_=warm[:, 0:1], func=ACT.Exp)
-        make_identity(nc, ident_b[:])
-        make_identity(nc, ident_f[:])
+        make_identity(nc, ident_bf16[:])
+        make_identity(nc, ident_f32[:])
 
-        nc.sync.dma_start(out=gh[:], in_=gate_hid)
-        nc.sync.dma_start(out=bz[0:1, 0 : 3 * C], in_=ba2.unsqueeze(0))
+        nc.sync.dma_start(out=gate_sb[:], in_=gate_hid)
+        nc.sync.dma_start(out=bias_rows[0:1, 0 : STREAMS * C], in_=ba2.unsqueeze(0))
         nc.sync.dma_start(out=wa2_sb[:], in_=wa2)
-        nc.sync.dma_start(out=bz[0:1, 3 * C : 4 * C], in_=bo.unsqueeze(0))
-        nc.sync.dma_start(out=wo_raw[:], in_=wo.rearrange("(t p) n -> p t n", p=P))
+        nc.sync.dma_start(out=bias_rows[0:1, STREAMS * C :], in_=bo.unsqueeze(0))
+        nc.sync.dma_start(out=wo_rows[:], in_=wo.rearrange("(t p) n -> p t n", p=P))
 
         x_tiles = {}
 
-        def load_chunk(c):
-            i0, n = chunks[c]
-            for k in range(3):
-                xt = xpool.tile([P, n, C], BF16, name="x%d_%d" % (k, c), tag="x%d" % k)
-                nc.sync.dma_start(out=xt[:], in_=xs[k][:, i0 : i0 + n, :])
-                x_tiles[(k, c)] = xt
+        def load_chunk(chunk):
+            first, n = span(chunk, CHUNK)
+            for k in range(STREAMS):
+                x = x_pool.tile([P, n, C], BF16, name="x%d_%d" % (k, chunk), tag="x%d" % k)
+                nc.sync.dma_start(out=x[:], in_=streams[k][:, first : first + n, :])
+                x_tiles[(k, chunk)] = x
 
-        for c in range(4):
-            load_chunk(c)
+        for chunk in range(4):
+            load_chunk(chunk)
 
         nc.gpsimd.tensor_scalar(
-            out=wo_grp[:],
-            in0=wo_raw[:].rearrange("p t n -> p n t"),
+            out=wo_grouped[:],
+            in0=wo_rows[:].rearrange("p t n -> p n t"),
             scalar1=1.0,
             scalar2=0.0,
             op0=ALU.mult,
             op1=ALU.add,
         )
 
-        tp = ps_o.tile([P, P], BF16, name="tp", tag="o")
-        nc.tensor.transpose(tp[:], gh[:], ident_b[:])
-        nc.vector.tensor_copy(out=gh_t[:], in_=tp[:])
+        flipped = psum_out.tile([P, P], BF16, name="flipped", tag="o")
+        nc.tensor.transpose(flipped[:], gate_sb[:], ident_bf16[:])
+        nc.vector.tensor_copy(out=gate_t[:], in_=flipped[:])
 
-        bz_k = bz[:, 0 : 3 * C].rearrange("g (c k) -> g k c", k=3)
-        wa2_k = wa2_sb[:].rearrange("g (c k) -> g k c", k=3)
-        z = [ps_f.tile([P, C], F32, name="z%d" % k, tag="f") for k in range(3)]
-        for k in range(3):
-            nc.tensor.matmul(z[k][:], lhsT=ones[:], rhs=bz_k[:, k, :], start=True, stop=False)
-        bo_ps = ps_o.tile([P, C], F32, name="bo_ps", tag="o")
-        nc.tensor.matmul(bo_ps[:], lhsT=ones[:], rhs=bz[:, 3 * C : 4 * C], start=True, stop=True)
-        for k in range(3):
-            nc.tensor.matmul(z[k][:], lhsT=gh_t[:], rhs=wa2_k[:, k, :], start=False, stop=True)
+        ba2_by_stream = bias_rows[:, 0 : STREAMS * C].rearrange("g (c k) -> g k c", k=STREAMS)
+        wa2_by_stream = wa2_sb[:].rearrange("g (c k) -> g k c", k=STREAMS)
+        z = [psum_sum.tile([P, C], F32, name="z%d" % k, tag="f") for k in range(STREAMS)]
+        for k in range(STREAMS):
+            nc.tensor.matmul(z[k][:], lhsT=ones[:], rhs=ba2_by_stream[:, k, :], start=True, stop=False)
+        bo_psum = psum_out.tile([P, C], F32, name="bo_psum", tag="o")
+        nc.tensor.matmul(bo_psum[:], lhsT=ones[:], rhs=bias_rows[:, STREAMS * C :], start=True, stop=True)
+        for k in range(STREAMS):
+            nc.tensor.matmul(z[k][:], lhsT=gate_t[:], rhs=wa2_by_stream[:, k, :], start=False, stop=True)
 
-        nc.scalar.copy(out=e[0][:], in_=z[0][:])
-        nc.vector.tensor_tensor(out=mx[:], in0=z[1][:], in1=e[0][:], op=ALU.max)
-        nc.vector.tensor_tensor(out=mx[:], in0=z[2][:], in1=mx[:], op=ALU.max)
-        nc.vector.tensor_tensor(out=e[2][:], in0=z[2][:], in1=mx[:], op=ALU.subtract)
-        nc.scalar.activation(out=e[2][:], in_=e[2][:], func=ACT.Exp)
-        nc.vector.tensor_tensor(out=e[0][:], in0=e[0][:], in1=mx[:], op=ALU.subtract)
-        nc.scalar.activation(out=e[0][:], in_=e[0][:], func=ACT.Exp)
-        nc.vector.tensor_tensor(out=e[1][:], in0=z[1][:], in1=mx[:], op=ALU.subtract)
-        nc.scalar.activation(out=e[1][:], in_=e[1][:], func=ACT.Exp)
-        nc.scalar.copy(out=bo_b[:], in_=bo_ps[:])
+        nc.scalar.copy(out=gate[0][:], in_=z[0][:])
+        nc.vector.tensor_tensor(out=top[:], in0=z[1][:], in1=gate[0][:], op=ALU.max)
+        nc.vector.tensor_tensor(out=top[:], in0=z[2][:], in1=top[:], op=ALU.max)
+        nc.vector.tensor_tensor(out=gate[2][:], in0=z[2][:], in1=top[:], op=ALU.subtract)
+        nc.scalar.activation(out=gate[2][:], in_=gate[2][:], func=ACT.Exp)
+        nc.vector.tensor_tensor(out=gate[0][:], in0=gate[0][:], in1=top[:], op=ALU.subtract)
+        nc.scalar.activation(out=gate[0][:], in_=gate[0][:], func=ACT.Exp)
+        nc.vector.tensor_tensor(out=gate[1][:], in0=z[1][:], in1=top[:], op=ALU.subtract)
+        nc.scalar.activation(out=gate[1][:], in_=gate[1][:], func=ACT.Exp)
+        nc.scalar.copy(out=bo_all[:], in_=bo_psum[:])
         nc.vector.quantize_mx(
             out=wo_codes[:].bitcast(FP8X4),
             scales=wo_scales[:],
-            in_=wo_grp[:].rearrange("p n t -> p (n t)"),
+            in_=wo_grouped[:].rearrange("p n t -> p (n t)"),
         )
-        nc.vector.tensor_tensor(out=sm[:], in0=e[2][:], in1=e[0][:], op=ALU.add)
-        nc.vector.tensor_tensor(out=sm[:], in0=sm[:], in1=e[1][:], op=ALU.add)
-        nc.vector.reciprocal(out=sm[:], in_=sm[:])
-        for k in (0, 1):
-            nc.vector.tensor_tensor(out=e[k][:], in0=e[k][:], in1=sm[:], op=ALU.mult)
-
-        a_ps = [ps_a.tile([P, C], F32, name="a_ps%d" % k, tag="a%d" % k) for k in range(2)]
+        nc.vector.tensor_tensor(out=total[:], in0=gate[2][:], in1=gate[0][:], op=ALU.add)
+        nc.vector.tensor_tensor(out=total[:], in0=total[:], in1=gate[1][:], op=ALU.add)
+        nc.vector.reciprocal(out=total[:], in_=total[:])
         for k in range(2):
-            tmp = ps_f.tile([P, T, P], F32, name="a_tmp%d" % k, tag="f")
-            for t in range(T):
-                nc.tensor.transpose(tmp[:, t, :], e[k][:, t * P : (t + 1) * P], ident_f[:])
-            nc.scalar.copy(out=a_t[k][:], in_=tmp[:])
+            nc.vector.tensor_tensor(out=gate[k][:], in0=gate[k][:], in1=total[:], op=ALU.mult)
+
+        gate_psum = [psum_gate.tile([P, C], F32, name="gate_psum%d" % k, tag="a%d" % k) for k in range(2)]
         for k in range(2):
-            for t in range(T):
-                nc.tensor.transpose(a_ps[k][:, t * P : (t + 1) * P], a_t[k][:, t, :], ident_f[:])
+            turned = psum_sum.tile([P, PACK, P], F32, name="turned%d" % k, tag="f")
+            for t in range(PACK):
+                nc.tensor.transpose(turned[:, t, :], gate[k][:, t * P : (t + 1) * P], ident_f32[:])
+            nc.scalar.copy(out=gate_flipped[k][:], in_=turned[:])
+        for k in range(2):
+            for t in range(PACK):
+                nc.tensor.transpose(gate_psum[k][:, t * P : (t + 1) * P], gate_flipped[k][:, t, :], ident_f32[:])
 
-        prod = {}
-        grp_t = {}
-        code_t = {}
-        o_t = {}
-        osb_t = {}
+        products = {}
+        grouped_tiles = {}
+        code_tiles = {}
+        out_banks = {}
+        out_tiles = {}
 
-        def gp_products(s):
-            i0, n = groups[s]
-            c = i0 // CHUNK
-            ks = [1, 2] if (i0 // BATCH) % 3 == 2 else [2]
-            for k in ks:
-                pt = ppool.tile([P, n, C], F32, name="pg%d_%d" % (k, i0), tag="pg%d" % k, bufs=(4 if k == 2 else 3))
-                nc.gpsimd.tensor_tensor(
-                    out=pt[:],
-                    in0=x_tiles[(k, c)][:, i0 - c * CHUNK : i0 - c * CHUNK + n, :],
-                    in1=e[k][:].unsqueeze(1).to_broadcast([P, n, C]),
-                    op=ALU.mult,
+        def multiply(engine, k, group, a_k, tag, bufs):
+            first, n = span(group, GROUP)
+            chunk = first // CHUNK
+            product = prod_pool.tile([P, n, C], F32, name="%s_%d" % (tag, group), tag=tag, bufs=bufs)
+            engine.tensor_tensor(
+                out=product[:],
+                in0=x_tiles[(k, chunk)][:, first % CHUNK : first % CHUNK + n, :],
+                in1=a_k[:].unsqueeze(1).to_broadcast([P, n, C]),
+                op=ALU.mult,
+            )
+            for j in range(n):
+                products[(k, first + j)] = (product, j)
+
+        def vector_products(group, a):
+            multiply(nc.vector, 0, group, a[0], "vector0", 3)
+            if not w_on_gpsimd(group * GROUP):
+                multiply(nc.vector, 1, group, a[1], "vector1", 3)
+
+        def gpsimd_products(group):
+            if w_on_gpsimd(group * GROUP):
+                multiply(nc.gpsimd, 1, group, gate[1], "gpsimd1", 3)
+            multiply(nc.gpsimd, 2, group, gate[2], "gpsimd2", 4)
+
+        def sum_transposed(group):
+            first, n = span(group, GROUP)
+            batch = first // BATCH
+            if first % BATCH == 0:
+                grouped_tiles[batch] = quant_pool.tile(
+                    [P, BATCH, P, PACK], BF16, name="grouped%d" % batch, tag="grouped", align_bytes=64
                 )
+            sums = [psum_sum.tile([P, PACK, P], F32, name="sum%d" % (first + j), tag="f") for j in range(n)]
+            for k in range(STREAMS):
                 for j in range(n):
-                    prod[(k, i0 + j)] = (pt, j)
-
-        def vec_products(s):
-            i0, n = groups[s]
-            c = i0 // CHUNK
-            ks = [0] if (i0 // BATCH) % 3 == 2 else [0, 1]
-            for k in ks:
-                pt = ppool.tile([P, n, C], F32, name="pv%d_%d" % (k, i0), tag="pv%d" % k)
-                a_src = a_ps[k] if s >= PSUM_A_FROM else e[k]
-                nc.vector.tensor_tensor(
-                    out=pt[:],
-                    in0=x_tiles[(k, c)][:, i0 - c * CHUNK : i0 - c * CHUNK + n, :],
-                    in1=a_src[:].unsqueeze(1).to_broadcast([P, n, C]),
-                    op=ALU.mult,
-                )
-                for j in range(n):
-                    prod[(k, i0 + j)] = (pt, j)
-
-        def sum_transposed(s):
-            i0, n = groups[s]
-            c = i0 // CHUNK
-            if i0 % CHUNK == 0:
-                grp_t[c] = qpool.tile([P, CHUNK, P, T], BF16, name="grp%d" % c, tag="grp", align_bytes=64)
-            grp = grp_t[c]
-            fts = [ps_f.tile([P, T, P], F32, name="ft%d" % (i0 + j), tag="f") for j in range(n)]
-            for k in range(3):
-                for j in range(n):
-                    pt, jj = prod[(k, i0 + j)]
-                    for t in range(T):
+                    product, index = products[(k, first + j)]
+                    for t in range(PACK):
                         nc.tensor.matmul(
-                            fts[j][:, t, :],
-                            lhsT=pt[:, jj, t * P : (t + 1) * P],
-                            rhs=ident_f[:],
+                            sums[j][:, t, :],
+                            lhsT=product[:, index, t * P : (t + 1) * P],
+                            rhs=ident_f32[:],
                             is_transpose=True,
                             start=(k == 0 and t == 0),
-                            stop=(k == 2 and t == T - 1),
+                            stop=(k == STREAMS - 1 and t == PACK - 1),
                         )
             for j in range(n):
-                nc.scalar.copy(out=grp[:, i0 % CHUNK + j, :, :], in_=fts[j][:].rearrange("p t b -> p b t"))
+                nc.scalar.copy(
+                    out=grouped_tiles[batch][:, first % BATCH + j, :, :],
+                    in_=sums[j][:].rearrange("p t b -> p b t"),
+                )
 
-        def quantise(c):
-            n = chunks[c][1]
-            codes = qpool.tile([P, CHUNK * P], U32, name="codes%d" % c, tag="codes", align_bytes=64)
-            scales = qpool.tile([P, CHUNK * P], U8, name="scales%d" % c, tag="scales", align_bytes=64)
-            code_t[c] = (codes, scales)
+        def quantise(batch):
+            n = span(batch, BATCH)[1]
+            codes = quant_pool.tile([P, BATCH * P], U32, name="codes%d" % batch, tag="codes", align_bytes=64)
+            scales = quant_pool.tile([P, BATCH * P], U8, name="scales%d" % batch, tag="scales", align_bytes=64)
+            code_tiles[batch] = (codes, scales)
             nc.vector.quantize_mx(
                 out=codes[:, 0 : n * P].bitcast(FP8X4),
                 scales=scales[:, 0 : n * P],
-                in_=grp_t[c][:, 0:n, :, :].rearrange("p j b t -> p (j b t)"),
+                in_=grouped_tiles[batch][:, 0:n, :, :].rearrange("p j b t -> p (j b t)"),
             )
 
-        def project(s):
-            i0, n = groups[s]
-            codes, scales = code_t[i0 // CHUNK]
-            o_t[s] = []
-            for j in range(n):
-                o = ps_o.tile([P, C], F32, name="o%d" % (i0 + j), tag="o")
-                col = (i0 % CHUNK + j) * P
+        def project(group):
+            first, n = span(group, GROUP)
+            codes, scales = code_tiles[first // BATCH]
+            for position in range(first, first + n):
+                columns = slice((position % BATCH) * P, (position % BATCH + 1) * P)
+                bank = psum_out.tile([P, C], F32, name="bank%d" % position, tag="o")
                 nc.tensor.matmul_mx(
-                    out=o[:],
-                    lhsT=codes[:, col : col + P].bitcast(FP8X4),
-                    lhsT_scale=scales[:, col : col + P],
+                    out=bank[:],
+                    lhsT=codes[:, columns].bitcast(FP8X4),
+                    lhsT_scale=scales[:, columns],
                     rhs=wo_codes[:].bitcast(FP8X4),
                     rhs_scale=wo_scales[:],
                     start=True,
                     stop=True,
                 )
-                o_t[s].append(o)
+                out_banks[position] = bank
 
-        def add_bias(s):
-            i0, n = groups[s]
-            osb = opool.tile([P, GROUP, C], F32, name="osb%d" % s, tag="osb")
-            osb_t[s] = osb
+        def add_bias(group):
+            first, n = span(group, GROUP)
+            out_tiles[group] = out_pool.tile([P, GROUP, C], F32, name="out%d" % group, tag="out")
             for j in range(n):
-                nc.vector.tensor_tensor(out=osb[:, j, :], in0=o_t[s][j][:], in1=bo_b[:], op=ALU.add)
+                nc.vector.tensor_tensor(
+                    out=out_tiles[group][:, j, :], in0=out_banks[first + j][:], in1=bo_all[:], op=ALU.add
+                )
 
-        def store(s):
-            i0, n = groups[s]
-            nc.scalar.dma_start(out=out_v[:, i0 : i0 + n, :], in_=osb_t[s][:, 0:n, :])
+        def store(group):
+            first, n = span(group, GROUP)
+            nc.scalar.dma_start(out=out_rows[:, first : first + n, :], in_=out_tiles[group][:, 0:n, :])
 
-        vec_products(0)
-        nc.vector.tensor_tensor(out=e[2][:], in0=e[2][:], in1=sm[:], op=ALU.mult)
-        gp_products(0)
-        gp_products(1)
-        for s in range(n_groups + 6):
-            if s % 4 == 1 and 0 <= s // 4 - 1 < len(chunks):
-                quantise(s // 4 - 1)
-            if 0 <= s - 6 < n_groups:
-                add_bias(s - 6)
-            if 1 <= s < n_groups:
-                vec_products(s)
-            if s + 2 < n_groups:
-                gp_products(s + 2)
-            if s % 4 == 3 and s // 4 + 4 < len(chunks):
-                load_chunk(s // 4 + 4)
-            if 0 <= s - 1 < n_groups:
-                sum_transposed(s - 1)
-            if 0 <= s - 5 < n_groups:
-                project(s - 5)
-            if 0 <= s - 6 < n_groups:
-                store(s - 6)
+        vector_products(0, gate)
+        nc.vector.tensor_tensor(out=gate[2][:], in0=gate[2][:], in1=total[:], op=ALU.mult)
+        gpsimd_products(0)
+        gpsimd_products(1)
+
+        for step in range(n_groups + 5):
+            if step % 2 == 0 and 0 <= step // 2 - 2 < n_batches:
+                quantise(step // 2 - 2)
+            if 0 <= step - 5 < n_groups:
+                add_bias(step - 5)
+            if 1 <= step < n_groups:
+                vector_products(step, gate_psum)
+            if step + 2 < n_groups:
+                gpsimd_products(step + 2)
+            if step % 4 == 3 and step // 4 + 4 < n_chunks:
+                load_chunk(step // 4 + 4)
+            if 0 <= step - 1 < n_groups:
+                sum_transposed(step - 1)
+            if 0 <= step - 4 < n_groups:
+                project(step - 4)
+            if 0 <= step - 5 < n_groups:
+                store(step - 5)

@@ -219,15 +219,16 @@ def tile_hiremodule_pc_t_kernel(tc, h_mix, w_mix, c_proj, gate_hid, wa2, ba2, wo
             for position in range(first, first + n):
                 columns = slice((position % BATCH) * P, (position % BATCH + 1) * P)
                 bank = psum_out.tile([P, C], F32, name="bank%d" % position, tag="o")
-                nc.tensor.matmul_mx(
-                    out=bank[:],
-                    lhsT=codes[:, columns].bitcast(FP8X4),
-                    lhsT_scale=scales[:, columns],
-                    rhs=wo_codes[:].bitcast(FP8X4),
-                    rhs_scale=wo_scales[:],
-                    start=True,
-                    stop=True,
-                )
+                for issue in range(2):
+                    nc.tensor.matmul_mx(
+                        out=bank[:],
+                        lhsT=codes[:, columns].bitcast(FP8X4),
+                        lhsT_scale=scales[:, columns],
+                        rhs=wo_codes[:].bitcast(FP8X4),
+                        rhs_scale=wo_scales[:],
+                        start=True,
+                        stop=True,
+                    )
                 out_banks[position] = bank
 
         def add_bias(group):

from contextlib import ExitStack

import concourse.mybir as mybir
from concourse.masks import make_identity

FLOPS = 2 * 128 * 49 * 512 * 512 + 2 * 128 * 128 * 1536

F32 = mybir.dt.float32
BF16 = mybir.dt.bfloat16
I32 = mybir.dt.int32
U32 = mybir.dt.uint32
U8 = mybir.dt.uint8
FP8X4 = mybir.dt.float8_e4m3fn_x4
ALU = mybir.AluOpType
ACT = mybir.ActivationFunctionType

P = 128
C = 512
PACK = 4
STREAMS = 3
POSITIONS = 49
GROUP = 2
BATCH = 4
CHUNK = 8


def tile_hiremodule_pc_t_kernel(tc, h_mix, w_mix, c_proj, gate_hid, wa2, ba2, wo, bo, out):
    nc = tc.nc
    streams = [x.rearrange("b i j c -> b (i j) c") for x in (h_mix, w_mix, c_proj)]
    out_rows = out.rearrange("b i j c -> b (i j) c")

    n_chunks = (POSITIONS + CHUNK - 1) // CHUNK
    n_batches = (POSITIONS + BATCH - 1) // BATCH
    n_groups = (POSITIONS + GROUP - 1) // GROUP

    def span(index, size):
        return index * size, min(size, POSITIONS - index * size)

    def w_on_gpsimd(first):
        return (first // BATCH) % 3 == 2

    with ExitStack() as ctx:
        ctx.enter_context(tc.manual_schedule())
        const = ctx.enter_context(tc.tile_pool(name="const", bufs=1))
        x_pool = ctx.enter_context(tc.tile_pool(name="x", bufs=4))
        prod_pool = ctx.enter_context(tc.tile_pool(name="prod", bufs=3))
        quant_pool = ctx.enter_context(tc.tile_pool(name="quant", bufs=3))
        out_pool = ctx.enter_context(tc.tile_pool(name="outs", bufs=4))
        psum_gate = ctx.enter_context(tc.psum_pool(name="psum_gate", bufs=1))
        psum_sum = ctx.enter_context(tc.psum_pool(name="psum_sum", bufs=4))
        psum_out = ctx.enter_context(tc.psum_pool(name="psum_out", bufs=2))

        bias_rows = const.tile([P, STREAMS * C + C], BF16, name="bias_rows")
        ones = const.tile([P, P], BF16, name="ones")
        warm = const.tile([P, 2], F32, name="warm")
        ident_bf16 = const.tile([P, P], BF16, name="ident_bf16")
        ident_f32 = const.tile([P, P], F32, name="ident_f32")
        gate_sb = const.tile([P, P], BF16, name="gate_sb")
        gate_t = const.tile([P, P], BF16, name="gate_t")
        wa2_sb = const.tile([P, STREAMS * C], BF16, name="wa2_sb")
        wo_rows = const.tile([P, PACK, C], BF16, name="wo_rows")
        wo_grouped = const.tile([P, C, PACK], BF16, name="wo_grouped", align_bytes=64)
        wo_codes = const.tile([P, C], U32, name="wo_codes", align_bytes=64)
        wo_scales = const.tile([P, C], U8, name="wo_scales", align_bytes=64)
        bo_all = const.tile([P, C], F32, name="bo_all")
        gate = [const.tile([P, C], F32, name="gate%d" % k) for k in range(STREAMS)]
        top = const.tile([P, C], F32, name="top")
        total = const.tile([P, C], F32, name="total")
        gate_flipped = [const.tile([P, PACK, P], F32, name="gate_flipped%d" % k) for k in range(2)]

        nc.vector.memset(bias_rows[:].bitcast(I32), 0)
        nc.vector.memset(ones[:], 1.0)
        nc.vector.memset(warm[:, 0:1], 0.0)
        nc.scalar.activation(out=warm[:, 1:2], in_=warm[:, 0:1], func=ACT.Exp)
        make_identity(nc, ident_bf16[:])
        make_identity(nc, ident_f32[:])

        nc.sync.dma_start(out=gate_sb[:], in_=gate_hid)
        nc.sync.dma_start(out=bias_rows[0:1, 0 : STREAMS * C], in_=ba2.unsqueeze(0))
        nc.sync.dma_start(out=wa2_sb[:], in_=wa2)
        nc.sync.dma_start(out=bias_rows[0:1, STREAMS * C :], in_=bo.unsqueeze(0))
        nc.sync.dma_start(out=wo_rows[:], in_=wo.rearrange("(t p) n -> p t n", p=P))

        x_tiles = {}

        def load_chunk(chunk):
            first, n = span(chunk, CHUNK)
            for k in range(STREAMS):
                x = x_pool.tile([P, n, C], BF16, name="x%d_%d" % (k, chunk), tag="x%d" % k)
                nc.sync.dma_start(out=x[:], in_=streams[k][:, first : first + n, :])
                x_tiles[(k, chunk)] = x

        for chunk in range(4):
            load_chunk(chunk)

        nc.gpsimd.tensor_scalar(
            out=wo_grouped[:],
            in0=wo_rows[:].rearrange("p t n -> p n t"),
            scalar1=1.0,
            scalar2=0.0,
            op0=ALU.mult,
            op1=ALU.add,
        )

        flipped = psum_out.tile([P, P], BF16, name="flipped", tag="o")
        nc.tensor.transpose(flipped[:], gate_sb[:], ident_bf16[:])
        nc.vector.tensor_copy(out=gate_t[:], in_=flipped[:])

        ba2_by_stream = bias_rows[:, 0 : STREAMS * C].rearrange("g (c k) -> g k c", k=STREAMS)
        wa2_by_stream = wa2_sb[:].rearrange("g (c k) -> g k c", k=STREAMS)
        z = [psum_sum.tile([P, C], F32, name="z%d" % k, tag="f") for k in range(STREAMS)]
        for k in range(STREAMS):
            nc.tensor.matmul(z[k][:], lhsT=ones[:], rhs=ba2_by_stream[:, k, :], start=True, stop=False)
        bo_psum = psum_out.tile([P, C], F32, name="bo_psum", tag="o")
        nc.tensor.matmul(bo_psum[:], lhsT=ones[:], rhs=bias_rows[:, STREAMS * C :], start=True, stop=True)
        for k in range(STREAMS):
            nc.tensor.matmul(z[k][:], lhsT=gate_t[:], rhs=wa2_by_stream[:, k, :], start=False, stop=True)

        nc.scalar.copy(out=gate[0][:], in_=z[0][:])
        nc.vector.tensor_tensor(out=top[:], in0=z[1][:], in1=gate[0][:], op=ALU.max)
        nc.vector.tensor_tensor(out=top[:], in0=z[2][:], in1=top[:], op=ALU.max)
        nc.vector.tensor_tensor(out=gate[2][:], in0=z[2][:], in1=top[:], op=ALU.subtract)
        nc.scalar.activation(out=gate[2][:], in_=gate[2][:], func=ACT.Exp)
        nc.vector.tensor_tensor(out=gate[0][:], in0=gate[0][:], in1=top[:], op=ALU.subtract)
        nc.scalar.activation(out=gate[0][:], in_=gate[0][:], func=ACT.Exp)
        nc.vector.tensor_tensor(out=gate[1][:], in0=z[1][:], in1=top[:], op=ALU.subtract)
        nc.scalar.activation(out=gate[1][:], in_=gate[1][:], func=ACT.Exp)
        nc.scalar.copy(out=bo_all[:], in_=bo_psum[:])
        nc.vector.quantize_mx(
            out=wo_codes[:].bitcast(FP8X4),
            scales=wo_scales[:],
            in_=wo_grouped[:].rearrange("p n t -> p (n t)"),
        )
        nc.vector.tensor_tensor(out=total[:], in0=gate[2][:], in1=gate[0][:], op=ALU.add)
        nc.vector.tensor_tensor(out=total[:], in0=total[:], in1=gate[1][:], op=ALU.add)
        nc.vector.reciprocal(out=total[:], in_=total[:])
        for k in range(2):
            nc.vector.tensor_tensor(out=gate[k][:], in0=gate[k][:], in1=total[:], op=ALU.mult)

        gate_psum = [psum_gate.tile([P, C], F32, name="gate_psum%d" % k, tag="a%d" % k) for k in range(2)]
        for k in range(2):
            turned = psum_sum.tile([P, PACK, P], F32, name="turned%d" % k, tag="f")
            for t in range(PACK):
                nc.tensor.transpose(turned[:, t, :], gate[k][:, t * P : (t + 1) * P], ident_f32[:])
            nc.scalar.copy(out=gate_flipped[k][:], in_=turned[:])
        for k in range(2):
            for t in range(PACK):
                nc.tensor.transpose(gate_psum[k][:, t * P : (t + 1) * P], gate_flipped[k][:, t, :], ident_f32[:])

        products = {}
        grouped_tiles = {}
        code_tiles = {}
        out_banks = {}
        out_tiles = {}

        def multiply(engine, k, group, a_k, tag, bufs):
            first, n = span(group, GROUP)
            chunk = first // CHUNK
            product = prod_pool.tile([P, n, C], F32, name="%s_%d" % (tag, group), tag=tag, bufs=bufs)
            engine.tensor_tensor(
                out=product[:],
                in0=x_tiles[(k, chunk)][:, first % CHUNK : first % CHUNK + n, :],
                in1=a_k[:].unsqueeze(1).to_broadcast([P, n, C]),
                op=ALU.mult,
            )
            for j in range(n):
                products[(k, first + j)] = (product, j)

        def vector_products(group, a):
            multiply(nc.vector, 0, group, a[0], "vector0", 3)
            if not w_on_gpsimd(group * GROUP):
                multiply(nc.vector, 1, group, a[1], "vector1", 3)

        def gpsimd_products(group):
            if w_on_gpsimd(group * GROUP):
                multiply(nc.gpsimd, 1, group, gate[1], "gpsimd1", 3)
            multiply(nc.gpsimd, 2, group, gate[2], "gpsimd2", 4)

        def sum_transposed(group):
            first, n = span(group, GROUP)
            batch = first // BATCH
            if first % BATCH == 0:
                grouped_tiles[batch] = quant_pool.tile(
                    [P, BATCH, P, PACK], BF16, name="grouped%d" % batch, tag="grouped", align_bytes=64
                )
            sums = [psum_sum.tile([P, PACK, P], F32, name="sum%d" % (first + j), tag="f") for j in range(n)]
            for k in range(STREAMS):
                for j in range(n):
                    product, index = products[(k, first + j)]
                    for t in range(PACK):
                        nc.tensor.matmul(
                            sums[j][:, t, :],
                            lhsT=product[:, index, t * P : (t + 1) * P],
                            rhs=ident_f32[:],
                            is_transpose=True,
                            start=(k == 0 and t == 0),
                            stop=(k == STREAMS - 1 and t == PACK - 1),
                        )
            for j in range(n):
                nc.scalar.copy(
                    out=grouped_tiles[batch][:, first % BATCH + j, :, :],
                    in_=sums[j][:].rearrange("p t b -> p b t"),
                )

        def quantise(batch):
            n = span(batch, BATCH)[1]
            codes = quant_pool.tile([P, BATCH * P], U32, name="codes%d" % batch, tag="codes", align_bytes=64)
            scales = quant_pool.tile([P, BATCH * P], U8, name="scales%d" % batch, tag="scales", align_bytes=64)
            code_tiles[batch] = (codes, scales)
            nc.vector.quantize_mx(
                out=codes[:, 0 : n * P].bitcast(FP8X4),
                scales=scales[:, 0 : n * P],
                in_=grouped_tiles[batch][:, 0:n, :, :].rearrange("p j b t -> p (j b t)"),
            )

        def project(group):
            first, n = span(group, GROUP)
            codes, scales = code_tiles[first // BATCH]
            for position in range(first, first + n):
                columns = slice((position % BATCH) * P, (position % BATCH + 1) * P)
                bank = psum_out.tile([P, C], F32, name="bank%d" % position, tag="o")
                for issue in range(2):
                    nc.tensor.matmul_mx(
                        out=bank[:],
                        lhsT=codes[:, columns].bitcast(FP8X4),
                        lhsT_scale=scales[:, columns],
                        rhs=wo_codes[:].bitcast(FP8X4),
                        rhs_scale=wo_scales[:],
                        start=True,
                        stop=True,
                    )
                out_banks[position] = bank

        def add_bias(group):
            first, n = span(group, GROUP)
            out_tiles[group] = out_pool.tile([P, GROUP, C], F32, name="out%d" % group, tag="out")
            for j in range(n):
                nc.vector.tensor_tensor(
                    out=out_tiles[group][:, j, :], in0=out_banks[first + j][:], in1=bo_all[:], op=ALU.add
                )

        def store(group):
            first, n = span(group, GROUP)
            nc.scalar.dma_start(out=out_rows[:, first : first + n, :], in_=out_tiles[group][:, 0:n, :])

        vector_products(0, gate)
        nc.vector.tensor_tensor(out=gate[2][:], in0=gate[2][:], in1=total[:], op=ALU.mult)
        gpsimd_products(0)
        gpsimd_products(1)

        for step in range(n_groups + 5):
            if step % 2 == 0 and 0 <= step // 2 - 2 < n_batches:
                quantise(step // 2 - 2)
            if 0 <= step - 5 < n_groups:
                add_bias(step - 5)
            if 1 <= step < n_groups:
                vector_products(step, gate_psum)
            if step + 2 < n_groups:
                gpsimd_products(step + 2)
            if step % 4 == 3 and step // 4 + 4 < n_chunks:
                load_chunk(step // 4 + 4)
            if 0 <= step - 1 < n_groups:
                sum_transposed(step - 1)
            if 0 <= step - 4 < n_groups:
                project(step - 4)
            if 0 <= step - 5 < n_groups:
                store(step - 5)
